import numpy as np
import ml_dtypes


def mxq(x, axis, fmt="e4m3"):
    dtype, down = {"e4m3": (ml_dtypes.float8_e4m3fn, 7), "e5m2": (ml_dtypes.float8_e5m2, 14)}[fmt]
    v = np.moveaxis(np.asarray(x, np.float32).astype(ml_dtypes.bfloat16).astype(np.float64), axis, -1)
    blocks = v.reshape(v.shape[:-1] + (-1, 32))
    amax = np.abs(blocks).max(-1, keepdims=True)
    byte = np.maximum(np.where(amax > 0, np.frexp(amax)[1] - 1 + 127, 0) - down, 1)
    scale = np.exp2(byte - 127.0)
    codes = (blocks / scale).astype(np.float32).astype(dtype).astype(np.float64)
    return np.moveaxis((codes * scale).reshape(v.shape), -1, axis)


WIDE = False


def mx_kscale(k):
    if not WIDE:
        return np.ones(k)
    levels = np.array([10, -10, 5, -5, 0])
    a = np.random.permutation(np.resize(levels, k // 512 * 4)).reshape(k // 512, 4)
    idx = np.arange(k)
    return np.exp2(a[idx // 512, idx % 128 // 32])


BF16 = ml_dtypes.bfloat16


def bf(x):
    return np.asarray(x, np.float32).astype(BF16)


def f64(x):
    return np.asarray(x).astype(np.float64)


B, L, C, KS, NL, BH, R = 4, 256, 1024, 4, 2, 64, 4
OUT = 2 * BH * NL


def setup_inputs():
    s, t = mx_kscale(C), mx_kscale(C)
    return {"local_features": bf(np.random.standard_normal((B, L, C)) * s),
            "wt": bf(np.random.standard_normal((C, C, KS)) / np.sqrt(C) / s[:, None, None] * t[None, :, None]),
            "bt": bf(np.random.standard_normal(C) * 0.5 * t),
            "w1": bf(np.random.standard_normal((OUT, C)) / np.sqrt(C) / t[None, :]),
            "b1": bf(np.random.standard_normal(OUT) * 0.5)}


def reference(local_features, wt, bt, w1, b1):
    xq = mxq(f64(local_features), 2, "e4m3")
    wq = mxq(f64(wt), 0, "e4m3")
    up = xq @ wq.reshape(C, C * KS)
    up = up.reshape(B, L, C, KS).transpose(0, 2, 1, 3).reshape(B, C, L * KS) + f64(bt)[None, :, None]
    y = (mxq(f64(w1), 1, "e4m3") @ mxq(up, 1, "e4m3")) + f64(b1)[None, :, None]
    y = np.tile(y, (1, 1, R))
    y = y.reshape(B, NL, 2 * BH, L * KS * R)
    return np.ascontiguousarray(y.transpose(2, 0, 1, 3))

@@ -1,0 +1,237 @@
+from contextlib import ExitStack
+
+import concourse.mybir as mybir
+from concourse.masks import make_identity
+
+F32 = mybir.dt.float32
+BF16 = mybir.dt.bfloat16
+U32 = mybir.dt.uint32
+U8 = mybir.dt.uint8
+FP8X4 = mybir.dt.float8_e4m3fn_x4
+IDENTITY = mybir.ActivationFunctionType.Identity
+
+B, L, C, TAPS, OUT, REPEAT = 4, 256, 1024, 4, 256, 4
+P = 128
+PACK = 4
+K_PASS = P * PACK
+PASSES = C // K_PASS
+O_TILES = C // P
+OUT_TILES = OUT // P
+ROW_TILES = L // P
+HALVES = L // P
+W_COLS = 256
+W_CHUNKS = C // W_COLS
+W_AHEAD = 4
+W_SCALAR_COLS = 96
+
+FLOPS = 2 * B * L * C * C * TAPS + 2 * OUT * C * B * L * TAPS
+
+
+def tile_conditionalfeaturesupsample_t_kernel(tc, local_features, wt, bt, w1, b1, out):
+    nc = tc.nc
+    with ExitStack() as stack:
+        keep = stack.enter_context(tc.tile_pool(name="keep", bufs=1))
+        w_raw_pool = stack.enter_context(tc.tile_pool(name="w_raw", bufs=W_AHEAD))
+        w_grouped_pool = stack.enter_context(tc.tile_pool(name="w_grouped", bufs=2))
+        x_grouped_pool = stack.enter_context(tc.tile_pool(name="x_grouped", bufs=2))
+        planes_pool = stack.enter_context(tc.tile_pool(name="planes", bufs=3))
+        up_grouped_pool = stack.enter_context(tc.tile_pool(name="up_grouped", bufs=3))
+        up_codes_pool = stack.enter_context(tc.tile_pool(name="up_codes", bufs=2))
+        y_pool = stack.enter_context(tc.tile_pool(name="y", bufs=2))
+        acc_psum = stack.enter_context(tc.psum_pool(name="acc_psum", bufs=4))
+        y_psum = stack.enter_context(tc.psum_pool(name="y_psum", bufs=2))
+        tr_psum = stack.enter_context(tc.psum_pool(name="tr_psum", bufs=2))
+
+        x_raw = {}
+
+        def load_x(b):
+            x_tile = keep.tile([P, ROW_TILES * C], BF16, name="x_raw%d" % b)
+            nc.sync.dma_start(
+                out=x_tile[:].rearrange("p (r c) -> p r c", r=ROW_TILES),
+                in_=local_features[b].rearrange("(r p) c -> p r c", p=P),
+            )
+            x_raw[b] = x_tile
+
+        w_raw = {}
+
+        def load_w(chunk):
+            oc, h = divmod(chunk, PASSES)
+            w_tile = w_raw_pool.tile([P, PACK, W_COLS * TAPS], BF16, name="w_raw")
+            nc.sync.dma_start(
+                out=w_tile[:],
+                in_=wt[K_PASS * h : K_PASS * (h + 1), W_COLS * oc : W_COLS * (oc + 1), :].rearrange(
+                    "(p j) o k -> p j (o k)", j=PACK
+                ),
+            )
+            w_raw[chunk] = w_tile
+
+        load_x(0)
+        for chunk in range(W_AHEAD):
+            load_w(chunk)
+        for b in range(1, B):
+            load_x(b)
+
+        w1_raw = keep.tile([P, OUT_TILES, C], BF16)
+        nc.scalar.dma_start(out=w1_raw[:], in_=w1.rearrange("(n p) c -> p n c", p=P))
+        bias_rows = keep.tile([P, P], BF16)
+        nc.vector.memset(bias_rows[:], 0.0)
+        nc.scalar.dma_start(out=bias_rows[0:O_TILES, :], in_=bt.rearrange("(t p) -> t p", p=P))
+        nc.scalar.dma_start(
+            out=bias_rows[O_TILES : O_TILES + OUT_TILES, :], in_=b1.rearrange("(n p) -> n p", p=P)
+        )
+
+        ident_f32 = keep.tile([P, P], F32)
+        make_identity(nc, ident_f32[:])
+        ident_bf16 = keep.tile([P, P], BF16)
+        make_identity(nc, ident_bf16[:])
+
+        x_codes = keep.tile([P, B, PASSES, L], U32, align_bytes=64)
+        x_scales = keep.tile([P, B, PASSES, L], U8, align_bytes=64)
+        w_codes = keep.tile([P, W_CHUNKS, PASSES, TAPS, W_COLS], U32, align_bytes=64)
+        w_scales = keep.tile([P, W_CHUNKS, PASSES, TAPS, W_COLS], U8, align_bytes=64)
+        w1_codes = keep.tile([P, PASSES, OUT], U32, align_bytes=64)
+        w1_scales = keep.tile([P, PASSES, OUT], U8, align_bytes=64)
+        bias_cols = keep.tile([P, O_TILES + OUT_TILES], F32)
+
+        def prepare_x(b):
+            x_words = x_raw[b][:].bitcast(F32).rearrange(
+                "p (r h q u) -> p r h u q", r=ROW_TILES, h=PASSES, u=2
+            )
+            x_grouped = x_grouped_pool.tile([P, PASSES * L * PACK], BF16, align_bytes=64)
+            x_grouped_words = x_grouped[:].bitcast(F32).rearrange("p (h r u) -> p h r u", h=PASSES, u=2)
+            for h in range(PASSES):
+                x_t = tr_psum.tile([P, 2, L], F32, tag="tr")
+                for u in range(2):
+                    for r in range(ROW_TILES):
+                        nc.tensor.transpose(
+                            out=x_t[:, u, P * r : P * (r + 1)], in_=x_words[:, r, h, u, :], identity=ident_f32[:]
+                        )
+                nc.scalar.copy(out=x_grouped_words[:, h], in_=x_t[:].rearrange("p u r -> p r u"))
+            nc.vector.quantize_mx(
+                out=x_codes[:, b].rearrange("p h r -> p (h r)").bitcast(FP8X4),
+                scales=x_scales[:, b].rearrange("p h r -> p (h r)"),
+                in_=x_grouped[:],
+            )
+
+        def prepare_biases():
+            bias_t = tr_psum.tile([P, P], BF16, tag="tr")
+            nc.tensor.transpose(out=bias_t[:], in_=bias_rows[:], identity=ident_bf16[:])
+            nc.vector.tensor_copy(out=bias_cols[:], in_=bias_t[:, 0 : O_TILES + OUT_TILES])
+
+        def prepare_w1():
+            w1_grouped = keep.tile([P, PASSES, OUT, PACK], BF16, align_bytes=64)
+            for g in range(PASSES):
+                for n in range(OUT_TILES):
+                    w1_t = tr_psum.tile([P, PACK, P], BF16, tag="tr")
+                    for t in range(PACK):
+                        first = K_PASS * g + P * t
+                        nc.tensor.transpose(
+                            out=w1_t[:, t, :], in_=w1_raw[:, n, first : first + P], identity=ident_bf16[:]
+                        )
+                    nc.scalar.copy(
+                        out=w1_grouped[:, g, P * n : P * (n + 1), :], in_=w1_t[:].rearrange("p t r -> p r t")
+                    )
+            nc.vector.quantize_mx(
+                out=w1_codes[:].rearrange("p g r -> p (g r)").bitcast(FP8X4),
+                scales=w1_scales[:].rearrange("p g r -> p (g r)"),
+                in_=w1_grouped[:].rearrange("p g r t -> p (g r t)"),
+            )
+
+        def prepare_w(chunk):
+            oc, h = divmod(chunk, PASSES)
+            source = w_raw[chunk][:].rearrange("p j (o k) -> p k o j", k=TAPS)
+            w_grouped = w_grouped_pool.tile([P, TAPS, W_COLS, PACK], BF16, align_bytes=64)
+            split = W_COLS - W_SCALAR_COLS
+            nc.vector.tensor_copy(out=w_grouped[:, :, :split, :], in_=source[:, :, :split, :])
+            nc.scalar.copy(out=w_grouped[:, :, split:, :], in_=source[:, :, split:, :])
+            nc.vector.quantize_mx(
+                out=w_codes[:, oc, h].rearrange("p k o -> p (k o)").bitcast(FP8X4),
+                scales=w_scales[:, oc, h].rearrange("p k o -> p (k o)"),
+                in_=w_grouped[:].rearrange("p k o j -> p (k o j)"),
+            )
+
+        def first_product(b, o_tile, planes):
+            oc, s = divmod(o_tile, W_COLS // P)
+            cols = slice(P * s, P * (s + 1))
+            t = o_tile % PACK
+            for pair in range(TAPS // 2):
+                acc = acc_psum.tile([P, 2, L], F32, tag="acc")
+                for i in range(2):
+                    k = 2 * pair + i
+                    for h in range(PASSES):
+                        nc.tensor.matmul_mx(
+                            out=acc[:, i, :],
+                            lhsT=w_codes[:, oc, h, k, cols].bitcast(FP8X4),
+                            lhsT_scale=w_scales[:, oc, h, k, cols],
+                            rhs=x_codes[:, b, h, :].bitcast(FP8X4),
+                            rhs_scale=x_scales[:, b, h, :],
+                            start=(h == 0),
+                            stop=(h == PASSES - 1),
+                        )
+                nc.scalar.activation(
+                    out=planes[:, t].rearrange("p f k l -> p k f l")[:, 2 * pair : 2 * pair + 2],
+                    in_=acc[:].rearrange("p k (f l) -> p k f l", f=HALVES),
+                    func=IDENTITY,
+                    bias=bias_cols[:, o_tile : o_tile + 1],
+                )
+
+        def quantise_up(g, half, planes, up_codes, up_scales):
+            up_grouped = up_grouped_pool.tile([P, TAPS * P, PACK], BF16, align_bytes=64)
+            nc.vector.tensor_copy(
+                out=up_grouped[:].rearrange("p (c i) t -> p c t i", i=4),
+                in_=planes[:, :, half].rearrange("p t k l -> p t (k l)").rearrange("p t (c i) -> p c t i", i=4),
+            )
+            nc.vector.quantize_mx(
+                out=up_codes[:, g, half, :].bitcast(FP8X4),
+                scales=up_scales[:, g, half, :],
+                in_=up_grouped[:].rearrange("p c t -> p (c t)"),
+            )
+
+        def second_product(half, up_codes, up_scales, y_sb):
+            for n in range(OUT_TILES):
+                y_acc = y_psum.tile([P, TAPS, P], F32, tag="y")
+                for g in range(PASSES):
+                    nc.tensor.matmul_mx(
+                        out=y_acc[:].rearrange("p k l -> p (k l)"),
+                        lhsT=w1_codes[:, g, P * n : P * (n + 1)].bitcast(FP8X4),
+                        lhsT_scale=w1_scales[:, g, P * n : P * (n + 1)],
+                        rhs=up_codes[:, g, half, :].bitcast(FP8X4),
+                        rhs_scale=up_scales[:, g, half, :],
+                        start=(g == 0),
+                        stop=(g == PASSES - 1),
+                    )
+                nc.vector.tensor_scalar_add(
+                    out=y_sb[:, n, half].rearrange("p (l k) -> p l k", k=TAPS),
+                    in0=y_acc[:].rearrange("p k l -> p l k"),
+                    scalar1=bias_cols[:, O_TILES + n : O_TILES + n + 1],
+                )
+
+        prepare_x(0)
+        prepare_biases()
+        prepare_w1()
+        for b in range(B):
+            up_codes = up_codes_pool.tile([P, PASSES, HALVES, TAPS * P], U32, align_bytes=64)
+            up_scales = up_codes_pool.tile([P, PASSES, HALVES, TAPS * P], U8, align_bytes=64)
+            y_sb = y_pool.tile([P, OUT_TILES, HALVES, TAPS * P], F32)
+            for g in range(PASSES):
+                planes = planes_pool.tile([P, PACK, HALVES, TAPS, P], BF16)
+                for t in range(PACK):
+                    o_tile = PACK * g + t
+                    if b == 0 and o_tile % (W_COLS // P) == 0:
+                        for h in range(PASSES):
+                            chunk = PASSES * (o_tile // (W_COLS // P)) + h
+                            prepare_w(chunk)
+                            if chunk + W_AHEAD < W_CHUNKS * PASSES:
+                                load_w(chunk + W_AHEAD)
+                    first_product(b, o_tile, planes)
+                if g == 0 and b + 1 < B:
+                    prepare_x(b + 1)
+                for half in range(HALVES):
+                    quantise_up(g, half, planes, up_codes, up_scales)
+            for half in range(HALVES):
+                second_product(half, up_codes, up_scales, y_sb)
+            for r in range(REPEAT):
+                nc.sync.dma_start(
+                    out=out[:, b, :, L * TAPS * r : L * TAPS * (r + 1)],
+                    in_=y_sb[:].rearrange("p n f c -> p n (f c)"),
+                )

@@ -139,11 +139,12 @@ def tile_conditionalfeaturesupsample_t_kernel(tc, local_features, wt, bt, w1, b1
 
         def prepare_w(chunk):
             oc, h = divmod(chunk, PASSES)
-            source = w_raw[chunk][:].rearrange("p j (o k) -> p k o j", k=TAPS)
+            source = w_raw[chunk][:].rearrange("p j (o k) -> p o j k", k=TAPS)
             w_grouped = w_grouped_pool.tile([P, TAPS, W_COLS, PACK], BF16, align_bytes=64)
+            target = w_grouped[:].rearrange("p k o j -> p o j k")
             split = W_COLS - W_SCALAR_COLS
-            nc.vector.tensor_copy(out=w_grouped[:, :, :split, :], in_=source[:, :, :split, :])
-            nc.scalar.copy(out=w_grouped[:, :, split:, :], in_=source[:, :, split:, :])
+            nc.vector.tensor_copy(out=target[:, :split], in_=source[:, :split])
+            nc.scalar.copy(out=target[:, split:], in_=source[:, split:])
             nc.vector.quantize_mx(
                 out=w_codes[:, oc, h].rearrange("p k o -> p (k o)").bitcast(FP8X4),
                 scales=w_scales[:, oc, h].rearrange("p k o -> p (k o)"),

@@ -32,10 +32,10 @@ def tile_conditionalfeaturesupsample_t_kernel(tc, local_features, wt, bt, w1, b1
     with ExitStack() as stack:
         keep = stack.enter_context(tc.tile_pool(name="keep", bufs=1))
         w_raw_pool = stack.enter_context(tc.tile_pool(name="w_raw", bufs=W_AHEAD))
-        w_grouped_pool = stack.enter_context(tc.tile_pool(name="w_grouped", bufs=2))
+        w_grouped_pool = stack.enter_context(tc.tile_pool(name="w_grouped", bufs=3))
         x_grouped_pool = stack.enter_context(tc.tile_pool(name="x_grouped", bufs=2))
         planes_pool = stack.enter_context(tc.tile_pool(name="planes", bufs=3))
-        up_grouped_pool = stack.enter_context(tc.tile_pool(name="up_grouped", bufs=3))
+        up_grouped_pool = stack.enter_context(tc.tile_pool(name="up_grouped", bufs=4))
         up_codes_pool = stack.enter_context(tc.tile_pool(name="up_codes", bufs=2))
         y_pool = stack.enter_context(tc.tile_pool(name="y", bufs=2))
         acc_psum = stack.enter_context(tc.psum_pool(name="acc_psum", bufs=4))
@@ -137,14 +137,20 @@ def tile_conditionalfeaturesupsample_t_kernel(tc, local_features, wt, bt, w1, b1
                 in_=w1_grouped[:].rearrange("p g r t -> p (g r t)"),
             )
 
-        def prepare_w(chunk):
-            oc, h = divmod(chunk, PASSES)
+        w_grouped_of = {}
+
+        def group_w(chunk):
             source = w_raw[chunk][:].rearrange("p j (o k) -> p o j k", k=TAPS)
             w_grouped = w_grouped_pool.tile([P, TAPS, W_COLS, PACK], BF16, align_bytes=64)
             target = w_grouped[:].rearrange("p k o j -> p o j k")
             split = W_COLS - W_SCALAR_COLS
             nc.vector.tensor_copy(out=target[:, :split], in_=source[:, :split])
             nc.scalar.copy(out=target[:, split:], in_=source[:, split:])
+            w_grouped_of[chunk] = w_grouped
+
+        def quantise_w(chunk):
+            oc, h = divmod(chunk, PASSES)
+            w_grouped = w_grouped_of[chunk]
             nc.vector.quantize_mx(
                 out=w_codes[:, oc, h].rearrange("p k o -> p (k o)").bitcast(FP8X4),
                 scales=w_scales[:, oc, h].rearrange("p k o -> p (k o)"),
@@ -176,17 +182,21 @@ def tile_conditionalfeaturesupsample_t_kernel(tc, local_features, wt, bt, w1, b1
                     bias=bias_cols[:, o_tile : o_tile + 1],
                 )
 
-        def quantise_up(g, half, planes, up_codes, up_scales):
-            up_grouped = up_grouped_pool.tile([P, TAPS * P, PACK], BF16, align_bytes=64)
-            nc.vector.tensor_copy(
-                out=up_grouped[:].rearrange("p (c i) t -> p c t i", i=4),
-                in_=planes[:, :, half].rearrange("p t k l -> p t (k l)").rearrange("p t (c i) -> p c t i", i=4),
-            )
-            nc.vector.quantize_mx(
-                out=up_codes[:, g, half, :].bitcast(FP8X4),
-                scales=up_scales[:, g, half, :],
-                in_=up_grouped[:].rearrange("p c t -> p (c t)"),
-            )
+        def quantise_up(g, planes, up_codes, up_scales):
+            grouped_halves = []
+            for half in range(HALVES):
+                up_grouped = up_grouped_pool.tile([P, TAPS * P, PACK], BF16, align_bytes=64)
+                nc.vector.tensor_copy(
+                    out=up_grouped[:].rearrange("p (c i) t -> p c t i", i=4),
+                    in_=planes[:, :, half].rearrange("p t k l -> p t (k l)").rearrange("p t (c i) -> p c t i", i=4),
+                )
+                grouped_halves.append(up_grouped)
+            for half in range(HALVES):
+                nc.vector.quantize_mx(
+                    out=up_codes[:, g, half, :].bitcast(FP8X4),
+                    scales=up_scales[:, g, half, :],
+                    in_=grouped_halves[half][:].rearrange("p c t -> p (c t)"),
+                )
 
         def second_product(half, up_codes, up_scales, y_sb):
             for n in range(OUT_TILES):
@@ -201,15 +211,18 @@ def tile_conditionalfeaturesupsample_t_kernel(tc, local_features, wt, bt, w1, b1
                         start=(g == 0),
                         stop=(g == PASSES - 1),
                     )
-                nc.vector.tensor_scalar_add(
-                    out=y_sb[:, n, half].rearrange("p (l k) -> p l k", k=TAPS),
-                    in0=y_acc[:].rearrange("p k l -> p l k"),
-                    scalar1=bias_cols[:, O_TILES + n : O_TILES + n + 1],
-                )
+                y_out = y_sb[:, n, half].rearrange("p (l k) -> p l k", k=TAPS)
+                y_in = y_acc[:].rearrange("p k l -> p l k")
+                y_bias = bias_cols[:, O_TILES + n : O_TILES + n + 1]
+                if n % 2 == 0:
+                    nc.vector.tensor_scalar_add(out=y_out, in0=y_in, scalar1=y_bias)
+                else:
+                    nc.scalar.activation(out=y_out, in_=y_in, func=IDENTITY, bias=y_bias)
 
+        time_steps = L * TAPS
         prepare_x(0)
         prepare_biases()
-        prepare_w1()
+        group_w(0)
         for b in range(B):
             up_codes = up_codes_pool.tile([P, PASSES, HALVES, TAPS * P], U32, align_bytes=64)
             up_scales = up_codes_pool.tile([P, PASSES, HALVES, TAPS * P], U8, align_bytes=64)
@@ -221,18 +234,31 @@ def tile_conditionalfeaturesupsample_t_kernel(tc, local_features, wt, bt, w1, b1
                     if b == 0 and o_tile % (W_COLS // P) == 0:
                         for h in range(PASSES):
                             chunk = PASSES * (o_tile // (W_COLS // P)) + h
-                            prepare_w(chunk)
+                            if chunk + 1 < W_CHUNKS * PASSES:
+                                group_w(chunk + 1)
+                            quantise_w(chunk)
                             if chunk + W_AHEAD < W_CHUNKS * PASSES:
                                 load_w(chunk + W_AHEAD)
                     first_product(b, o_tile, planes)
                 if g == 0 and b + 1 < B:
                     prepare_x(b + 1)
+                if g == 0 and b == 0:
+                    prepare_w1()
+                quantise_up(g, planes, up_codes, up_scales)
+            if b + 1 < B:
                 for half in range(HALVES):
-                    quantise_up(g, half, planes, up_codes, up_scales)
-            for half in range(HALVES):
-                second_product(half, up_codes, up_scales, y_sb)
-            for r in range(REPEAT):
-                nc.sync.dma_start(
-                    out=out[:, b, :, L * TAPS * r : L * TAPS * (r + 1)],
-                    in_=y_sb[:].rearrange("p n f c -> p n (f c)"),
-                )
+                    second_product(half, up_codes, up_scales, y_sb)
+                for r in range(REPEAT):
+                    nc.sync.dma_start(
+                        out=out[:, b, :, time_steps * r : time_steps * (r + 1)],
+                        in_=y_sb[:].rearrange("p n f c -> p n (f c)"),
+                    )
+            else:
+                for half in range(HALVES):
+                    second_product(half, up_codes, up_scales, y_sb)
+                    first = TAPS * P * half
+                    for r in range(REPEAT):
+                        nc.sync.dma_start(
+                            out=out[:, b, :, time_steps * r + first : time_steps * r + first + TAPS * P],
+                            in_=y_sb[:, :, half, :],
+                        )

@@ -11,18 +11,24 @@ FP8X4 = mybir.dt.float8_e4m3fn_x4
 IDENTITY = mybir.ActivationFunctionType.Identity
 
 B, L, C, TAPS, OUT, REPEAT = 4, 256, 1024, 4, 256, 4
+T_OUT = L * TAPS
 P = 128
 PACK = 4
+PAIR = 2
 K_PASS = P * PACK
 PASSES = C // K_PASS
+BANK = 512
 O_TILES = C // P
 OUT_TILES = OUT // P
-ROW_TILES = L // P
 HALVES = L // P
 W_COLS = 256
-W_CHUNKS = C // W_COLS
-W_AHEAD = 4
-W_SCALAR_COLS = 96
+W_TILES = W_COLS // P
+W_CHUNKS = (C // W_COLS) * PASSES
+RUN = 4
+
+W_SCALAR_COLS = 80
+RAW_BUFS = 6
+WHOLE_BATCHES = 2
 
 FLOPS = 2 * B * L * C * C * TAPS + 2 * OUT * C * B * L * TAPS
 
@@ -31,48 +37,54 @@ def tile_conditionalfeaturesupsample_t_kernel(tc, local_features, wt, bt, w1, b1
     nc = tc.nc
     with ExitStack() as stack:
         keep = stack.enter_context(tc.tile_pool(name="keep", bufs=1))
-        w_raw_pool = stack.enter_context(tc.tile_pool(name="w_raw", bufs=W_AHEAD))
+        raw_pool = stack.enter_context(tc.tile_pool(name="raw", bufs=RAW_BUFS))
         w_grouped_pool = stack.enter_context(tc.tile_pool(name="w_grouped", bufs=3))
         x_grouped_pool = stack.enter_context(tc.tile_pool(name="x_grouped", bufs=2))
         planes_pool = stack.enter_context(tc.tile_pool(name="planes", bufs=3))
-        up_grouped_pool = stack.enter_context(tc.tile_pool(name="up_grouped", bufs=4))
+        up_grouped_pool = stack.enter_context(tc.tile_pool(name="up_grouped", bufs=2 * HALVES))
         up_codes_pool = stack.enter_context(tc.tile_pool(name="up_codes", bufs=2))
-        y_pool = stack.enter_context(tc.tile_pool(name="y", bufs=2))
+        y_pool = stack.enter_context(tc.tile_pool(name="y", bufs=3))
         acc_psum = stack.enter_context(tc.psum_pool(name="acc_psum", bufs=4))
         y_psum = stack.enter_context(tc.psum_pool(name="y_psum", bufs=2))
         tr_psum = stack.enter_context(tc.psum_pool(name="tr_psum", bufs=2))
 
-        x_raw = {}
+        ring_order = [("x", 0)]
+        ring_order.extend([("wt", chunk) for chunk in range(W_CHUNKS // 2)])
+        ring_order.append(("x", 1))
+        ring_order.extend([("wt", chunk) for chunk in range(W_CHUNKS // 2, W_CHUNKS)])
+        ring_order.append(("w1", 0))
+        ring_order.extend([("x", b) for b in range(2, B)])
+        raw = {}
 
-        def load_x(b):
-            x_tile = keep.tile([P, ROW_TILES * C], BF16, name="x_raw%d" % b)
-            nc.sync.dma_start(
-                out=x_tile[:].rearrange("p (r c) -> p r c", r=ROW_TILES),
-                in_=local_features[b].rearrange("(r p) c -> p r c", p=P),
-            )
-            x_raw[b] = x_tile
+        def load_next():
+            if len(raw) == len(ring_order):
+                return
+            name, index = ring_order[len(raw)]
+            if name == "x":
+                x_raw = raw_pool.tile([P, HALVES * C], BF16, tag="raw")
+                nc.sync.dma_start(
+                    out=x_raw[:].rearrange("p (r c) -> p r c", r=HALVES),
+                    in_=local_features[index].rearrange("(r p) c -> p r c", p=P),
+                )
+                raw[name, index] = x_raw
+            elif name == "wt":
+                oc, h = divmod(index, PASSES)
+                w_raw = raw_pool.tile([P, PACK, W_COLS * TAPS], BF16, tag="raw")
+                nc.sync.dma_start(
+                    out=w_raw[:],
+                    in_=wt[K_PASS * h : K_PASS * (h + 1), W_COLS * oc : W_COLS * (oc + 1), :].rearrange(
+                        "(p j) o k -> p j (o k)", j=PACK
+                    ),
+                )
+                raw[name, index] = w_raw
+            else:
+                w1_raw = raw_pool.tile([P, OUT_TILES, C], BF16, tag="raw")
+                nc.sync.dma_start(out=w1_raw[:], in_=w1.rearrange("(n p) c -> p n c", p=P))
+                raw[name, index] = w1_raw
 
-        w_raw = {}
+        for slot in range(RAW_BUFS):
+            load_next()
 
-        def load_w(chunk):
-            oc, h = divmod(chunk, PASSES)
-            w_tile = w_raw_pool.tile([P, PACK, W_COLS * TAPS], BF16, name="w_raw")
-            nc.sync.dma_start(
-                out=w_tile[:],
-                in_=wt[K_PASS * h : K_PASS * (h + 1), W_COLS * oc : W_COLS * (oc + 1), :].rearrange(
-                    "(p j) o k -> p j (o k)", j=PACK
-                ),
-            )
-            w_raw[chunk] = w_tile
-
-        load_x(0)
-        for chunk in range(W_AHEAD):
-            load_w(chunk)
-        for b in range(1, B):
-            load_x(b)
-
-        w1_raw = keep.tile([P, OUT_TILES, C], BF16)
-        nc.scalar.dma_start(out=w1_raw[:], in_=w1.rearrange("(n p) c -> p n c", p=P))
         bias_rows = keep.tile([P, P], BF16)
         nc.vector.memset(bias_rows[:], 0.0)
         nc.scalar.dma_start(out=bias_rows[0:O_TILES, :], in_=bt.rearrange("(t p) -> t p", p=P))
@@ -87,26 +99,27 @@ def tile_conditionalfeaturesupsample_t_kernel(tc, local_features, wt, bt, w1, b1
 
         x_codes = keep.tile([P, B, PASSES, L], U32, align_bytes=64)
         x_scales = keep.tile([P, B, PASSES, L], U8, align_bytes=64)
-        w_codes = keep.tile([P, W_CHUNKS, PASSES, TAPS, W_COLS], U32, align_bytes=64)
-        w_scales = keep.tile([P, W_CHUNKS, PASSES, TAPS, W_COLS], U8, align_bytes=64)
+        w_codes = keep.tile([P, W_CHUNKS, TAPS, W_COLS], U32, align_bytes=64)
+        w_scales = keep.tile([P, W_CHUNKS, TAPS, W_COLS], U8, align_bytes=64)
         w1_codes = keep.tile([P, PASSES, OUT], U32, align_bytes=64)
         w1_scales = keep.tile([P, PASSES, OUT], U8, align_bytes=64)
         bias_cols = keep.tile([P, O_TILES + OUT_TILES], F32)
 
         def prepare_x(b):
-            x_words = x_raw[b][:].bitcast(F32).rearrange(
-                "p (r h q u) -> p r h u q", r=ROW_TILES, h=PASSES, u=2
+            x_words = raw["x", b][:].bitcast(F32).rearrange(
+                "p (r h q u) -> p r h u q", r=HALVES, h=PASSES, u=PAIR
             )
             x_grouped = x_grouped_pool.tile([P, PASSES * L * PACK], BF16, align_bytes=64)
-            x_grouped_words = x_grouped[:].bitcast(F32).rearrange("p (h r u) -> p h r u", h=PASSES, u=2)
+            x_grouped_words = x_grouped[:].bitcast(F32).rearrange("p (h r u) -> p h r u", h=PASSES, u=PAIR)
             for h in range(PASSES):
-                x_t = tr_psum.tile([P, 2, L], F32, tag="tr")
-                for u in range(2):
-                    for r in range(ROW_TILES):
+                x_t = tr_psum.tile([P, PAIR, L], F32, tag="tr")
+                for u in range(PAIR):
+                    for r in range(HALVES):
                         nc.tensor.transpose(
                             out=x_t[:, u, P * r : P * (r + 1)], in_=x_words[:, r, h, u, :], identity=ident_f32[:]
                         )
                 nc.scalar.copy(out=x_grouped_words[:, h], in_=x_t[:].rearrange("p u r -> p r u"))
+            load_next()
             nc.vector.quantize_mx(
                 out=x_codes[:, b].rearrange("p h r -> p (h r)").bitcast(FP8X4),
                 scales=x_scales[:, b].rearrange("p h r -> p (h r)"),
@@ -119,18 +132,20 @@ def tile_conditionalfeaturesupsample_t_kernel(tc, local_features, wt, bt, w1, b1
             nc.vector.tensor_copy(out=bias_cols[:], in_=bias_t[:, 0 : O_TILES + OUT_TILES])
 
         def prepare_w1():
+            w1_raw = raw["w1", 0]
             w1_grouped = keep.tile([P, PASSES, OUT, PACK], BF16, align_bytes=64)
             for g in range(PASSES):
                 for n in range(OUT_TILES):
                     w1_t = tr_psum.tile([P, PACK, P], BF16, tag="tr")
                     for t in range(PACK):
-                        first = K_PASS * g + P * t
+                        first_o = K_PASS * g + P * t
                         nc.tensor.transpose(
-                            out=w1_t[:, t, :], in_=w1_raw[:, n, first : first + P], identity=ident_bf16[:]
+                            out=w1_t[:, t, :], in_=w1_raw[:, n, first_o : first_o + P], identity=ident_bf16[:]
                         )
                     nc.scalar.copy(
                         out=w1_grouped[:, g, P * n : P * (n + 1), :], in_=w1_t[:].rearrange("p t r -> p r t")
                     )
+            load_next()
             nc.vector.quantize_mx(
                 out=w1_codes[:].rearrange("p g r -> p (g r)").bitcast(FP8X4),
                 scales=w1_scales[:].rearrange("p g r -> p (g r)"),
@@ -140,65 +155,67 @@ def tile_conditionalfeaturesupsample_t_kernel(tc, local_features, wt, bt, w1, b1
         w_grouped_of = {}
 
         def group_w(chunk):
-            source = w_raw[chunk][:].rearrange("p j (o k) -> p o j k", k=TAPS)
+            source = raw["wt", chunk][:].rearrange("p j (o k) -> p o j k", k=TAPS)
             w_grouped = w_grouped_pool.tile([P, TAPS, W_COLS, PACK], BF16, align_bytes=64)
             target = w_grouped[:].rearrange("p k o j -> p o j k")
             split = W_COLS - W_SCALAR_COLS
             nc.vector.tensor_copy(out=target[:, :split], in_=source[:, :split])
             nc.scalar.copy(out=target[:, split:], in_=source[:, split:])
             w_grouped_of[chunk] = w_grouped
+            load_next()
 
         def quantise_w(chunk):
-            oc, h = divmod(chunk, PASSES)
-            w_grouped = w_grouped_of[chunk]
             nc.vector.quantize_mx(
-                out=w_codes[:, oc, h].rearrange("p k o -> p (k o)").bitcast(FP8X4),
-                scales=w_scales[:, oc, h].rearrange("p k o -> p (k o)"),
-                in_=w_grouped[:].rearrange("p k o j -> p (k o j)"),
+                out=w_codes[:, chunk].rearrange("p k o -> p (k o)").bitcast(FP8X4),
+                scales=w_scales[:, chunk].rearrange("p k o -> p (k o)"),
+                in_=w_grouped_of[chunk][:].rearrange("p k o j -> p (k o j)"),
             )
 
-        def first_product(b, o_tile, planes):
-            oc, s = divmod(o_tile, W_COLS // P)
-            cols = slice(P * s, P * (s + 1))
+        def first_product(b, first_half, halves, o_tile, planes):
+            oc, s = divmod(o_tile, W_TILES)
+            o_cols = slice(P * s, P * (s + 1))
+            width = P * halves
+            x_cols = slice(P * first_half, P * first_half + width)
+            taps_in_bank = BANK // width
             t = o_tile % PACK
-            for pair in range(TAPS // 2):
-                acc = acc_psum.tile([P, 2, L], F32, tag="acc")
-                for i in range(2):
-                    k = 2 * pair + i
+            for k0 in range(0, TAPS, taps_in_bank):
+                acc = acc_psum.tile([P, taps_in_bank, width], F32, tag="acc")
+                for i in range(taps_in_bank):
                     for h in range(PASSES):
+                        chunk = PASSES * oc + h
                         nc.tensor.matmul_mx(
                             out=acc[:, i, :],
-                            lhsT=w_codes[:, oc, h, k, cols].bitcast(FP8X4),
-                            lhsT_scale=w_scales[:, oc, h, k, cols],
-                            rhs=x_codes[:, b, h, :].bitcast(FP8X4),
-                            rhs_scale=x_scales[:, b, h, :],
+                            lhsT=w_codes[:, chunk, k0 + i, o_cols].bitcast(FP8X4),
+                            lhsT_scale=w_scales[:, chunk, k0 + i, o_cols],
+                            rhs=x_codes[:, b, h, x_cols].bitcast(FP8X4),
+                            rhs_scale=x_scales[:, b, h, x_cols],
                             start=(h == 0),
                             stop=(h == PASSES - 1),
                         )
                 nc.scalar.activation(
-                    out=planes[:, t].rearrange("p f k l -> p k f l")[:, 2 * pair : 2 * pair + 2],
-                    in_=acc[:].rearrange("p k (f l) -> p k f l", f=HALVES),
+                    out=planes[:, t, :, k0 : k0 + taps_in_bank, :].rearrange("p f k l -> p k f l"),
+                    in_=acc[:].rearrange("p k (f l) -> p k f l", f=halves),
                     func=IDENTITY,
                     bias=bias_cols[:, o_tile : o_tile + 1],
                 )
 
-        def quantise_up(g, planes, up_codes, up_scales):
+        def quantise_up(g, halves, planes, up_codes, up_scales):
             grouped_halves = []
-            for half in range(HALVES):
-                up_grouped = up_grouped_pool.tile([P, TAPS * P, PACK], BF16, align_bytes=64)
+            for f in range(halves):
+                up_grouped = up_grouped_pool.tile([P, BANK, PACK], BF16, align_bytes=64)
                 nc.vector.tensor_copy(
-                    out=up_grouped[:].rearrange("p (c i) t -> p c t i", i=4),
-                    in_=planes[:, :, half].rearrange("p t k l -> p t (k l)").rearrange("p t (c i) -> p c t i", i=4),
+                    out=up_grouped[:].rearrange("p (c i) t -> p c t i", i=RUN),
+                    in_=planes[:, :, f].rearrange("p t k l -> p t (k l)").rearrange("p t (c i) -> p c t i", i=RUN),
                 )
                 grouped_halves.append(up_grouped)
-            for half in range(HALVES):
+            for f in range(halves):
                 nc.vector.quantize_mx(
-                    out=up_codes[:, g, half, :].bitcast(FP8X4),
-                    scales=up_scales[:, g, half, :],
-                    in_=grouped_halves[half][:].rearrange("p c t -> p (c t)"),
+                    out=up_codes[:, g, f, :].bitcast(FP8X4),
+                    scales=up_scales[:, g, f, :],
+                    in_=grouped_halves[f][:].rearrange("p c t -> p (c t)"),
                 )
 
-        def second_product(half, up_codes, up_scales, y_sb):
+        def second_product(f, up_codes, up_scales, y_sb):
             for n in range(OUT_TILES):
                 y_acc = y_psum.tile([P, TAPS, P], F32, tag="y")
                 for g in range(PASSES):
@@ -206,12 +223,12 @@ def tile_conditionalfeaturesupsample_t_kernel(tc, local_features, wt, bt, w1, b1
                         out=y_acc[:].rearrange("p k l -> p (k l)"),
                         lhsT=w1_codes[:, g, P * n : P * (n + 1)].bitcast(FP8X4),
                         lhsT_scale=w1_scales[:, g, P * n : P * (n + 1)],
-                        rhs=up_codes[:, g, half, :].bitcast(FP8X4),
-                        rhs_scale=up_scales[:, g, half, :],
+                        rhs=up_codes[:, g, f, :].bitcast(FP8X4),
+                        rhs_scale=up_scales[:, g, f, :],
                         start=(g == 0),
                         stop=(g == PASSES - 1),
                     )
-                y_out = y_sb[:, n, half].rearrange("p (l k) -> p l k", k=TAPS)
+                y_out = y_sb[:, n, f].rearrange("p (l k) -> p l k", k=TAPS)
                 y_in = y_acc[:].rearrange("p k l -> p l k")
                 y_bias = bias_cols[:, O_TILES + n : O_TILES + n + 1]
                 if n % 2 == 0:
@@ -219,46 +236,42 @@ def tile_conditionalfeaturesupsample_t_kernel(tc, local_features, wt, bt, w1, b1
                 else:
                     nc.scalar.activation(out=y_out, in_=y_in, func=IDENTITY, bias=y_bias)
 
-        time_steps = L * TAPS
+        pieces = [(b, 0, HALVES) for b in range(WHOLE_BATCHES)]
+        pieces.extend([(b, half, 1) for b in range(WHOLE_BATCHES, B) for half in range(HALVES)])
         prepare_x(0)
         prepare_biases()
         group_w(0)
-        for b in range(B):
-            up_codes = up_codes_pool.tile([P, PASSES, HALVES, TAPS * P], U32, align_bytes=64)
-            up_scales = up_codes_pool.tile([P, PASSES, HALVES, TAPS * P], U8, align_bytes=64)
-            y_sb = y_pool.tile([P, OUT_TILES, HALVES, TAPS * P], F32)
+        for index, (b, first_half, halves) in enumerate(pieces):
+            up_codes = up_codes_pool.tile([P, PASSES, halves, BANK], U32, align_bytes=64, tag="up_codes")
+            up_scales = up_codes_pool.tile([P, PASSES, halves, BANK], U8, align_bytes=64, tag="up_scales")
+            y_sb = y_pool.tile([P, OUT_TILES, halves, BANK], F32, tag="y_sb")
+            planes_of = []
             for g in range(PASSES):
-                planes = planes_pool.tile([P, PACK, HALVES, TAPS, P], BF16)
+                planes = planes_pool.tile([P, PACK, halves, TAPS, P], BF16, tag="planes")
+                planes_of.append(planes)
                 for t in range(PACK):
                     o_tile = PACK * g + t
-                    if b == 0 and o_tile % (W_COLS // P) == 0:
+                    if index == 0 and o_tile % W_TILES == 0:
                         for h in range(PASSES):
-                            chunk = PASSES * (o_tile // (W_COLS // P)) + h
-                            if chunk + 1 < W_CHUNKS * PASSES:
+                            chunk = PASSES * (o_tile // W_TILES) + h
+                            if chunk + 1 < W_CHUNKS:
                                 group_w(chunk + 1)
                             quantise_w(chunk)
-                            if chunk + W_AHEAD < W_CHUNKS * PASSES:
-                                load_w(chunk + W_AHEAD)
-                    first_product(b, o_tile, planes)
-                if g == 0 and b + 1 < B:
+                    first_product(b, first_half, halves, o_tile, planes)
+                if g == 0 and first_half == 0 and b + 1 < B:
                     prepare_x(b + 1)
-                if g == 0 and b == 0:
+                if g == 1 and index == 0:
                     prepare_w1()
-                quantise_up(g, planes, up_codes, up_scales)
-            if b + 1 < B:
-                for half in range(HALVES):
-                    second_product(half, up_codes, up_scales, y_sb)
-                for r in range(REPEAT):
-                    nc.sync.dma_start(
-                        out=out[:, b, :, time_steps * r : time_steps * (r + 1)],
-                        in_=y_sb[:].rearrange("p n f c -> p n (f c)"),
-                    )
-            else:
-                for half in range(HALVES):
-                    second_product(half, up_codes, up_scales, y_sb)
-                    first = TAPS * P * half
-                    for r in range(REPEAT):
-                        nc.sync.dma_start(
-                            out=out[:, b, :, time_steps * r + first : time_steps * r + first + TAPS * P],
-                            in_=y_sb[:, :, half, :],
-                        )
+                if index > 0:
+                    quantise_up(g, halves, planes, up_codes, up_scales)
+            if index == 0:
+                for g in range(PASSES):
+                    quantise_up(g, halves, planes_of[g], up_codes, up_scales)
+            for f in range(halves):
+                second_product(f, up_codes, up_scales, y_sb)
+            first_t = BANK * first_half
+            for r in range(REPEAT):
+                nc.sync.dma_start(
+                    out=out[:, b, :, T_OUT * r + first_t : T_OUT * r + first_t + BANK * halves],
+                    in_=y_sb[:].rearrange("p n f c -> p n (f c)"),
+                )

@@ -29,6 +29,7 @@ RUN = 4
 W_SCALAR_COLS = 80
 RAW_BUFS = 6
 WHOLE_BATCHES = 2
+SECOND_AFTER = 4
 
 FLOPS = 2 * B * L * C * C * TAPS + 2 * OUT * C * B * L * TAPS
 
@@ -236,11 +237,22 @@ def tile_conditionalfeaturesupsample_t_kernel(tc, local_features, wt, bt, w1, b1
                 else:
                     nc.scalar.activation(out=y_out, in_=y_in, func=IDENTITY, bias=y_bias)
 
+        def finish(b, first_half, halves, up_codes, up_scales, y_sb):
+            for f in range(halves):
+                second_product(f, up_codes, up_scales, y_sb)
+            first_t = BANK * first_half
+            for r in range(REPEAT):
+                nc.sync.dma_start(
+                    out=out[:, b, :, T_OUT * r + first_t : T_OUT * r + first_t + BANK * halves],
+                    in_=y_sb[:].rearrange("p n f c -> p n (f c)"),
+                )
+
         pieces = [(b, 0, HALVES) for b in range(WHOLE_BATCHES)]
         pieces.extend([(b, half, 1) for b in range(WHOLE_BATCHES, B) for half in range(HALVES)])
         prepare_x(0)
         prepare_biases()
         group_w(0)
+        unfinished = []
         for index, (b, first_half, halves) in enumerate(pieces):
             up_codes = up_codes_pool.tile([P, PASSES, halves, BANK], U32, align_bytes=64, tag="up_codes")
             up_scales = up_codes_pool.tile([P, PASSES, halves, BANK], U8, align_bytes=64, tag="up_scales")
@@ -258,6 +270,8 @@ def tile_conditionalfeaturesupsample_t_kernel(tc, local_features, wt, bt, w1, b1
                                 group_w(chunk + 1)
                             quantise_w(chunk)
                     first_product(b, first_half, halves, o_tile, planes)
+                    if index > 0 and o_tile == SECOND_AFTER - 1:
+                        finish(*unfinished.pop())
                 if g == 0 and first_half == 0 and b + 1 < B:
                     prepare_x(b + 1)
                 if g == 1 and index == 0:
@@ -267,11 +281,5 @@ def tile_conditionalfeaturesupsample_t_kernel(tc, local_features, wt, bt, w1, b1
             if index == 0:
                 for g in range(PASSES):
                     quantise_up(g, halves, planes_of[g], up_codes, up_scales)
-            for f in range(halves):
-                second_product(f, up_codes, up_scales, y_sb)
-            first_t = BANK * first_half
-            for r in range(REPEAT):
-                nc.sync.dma_start(
-                    out=out[:, b, :, T_OUT * r + first_t : T_OUT * r + first_t + BANK * halves],
-                    in_=y_sb[:].rearrange("p n f c -> p n (f c)"),
-                )
+            unfinished.append((b, first_half, halves, up_codes, up_scales, y_sb))
+        finish(*unfinished.pop())

@@ -26,10 +26,9 @@ W_TILES = W_COLS // P
 W_CHUNKS = (C // W_COLS) * PASSES
 RUN = 4
 
-W_SCALAR_COLS = 80
+W_SCALAR_COLS = 48
 RAW_BUFS = 6
-WHOLE_BATCHES = 2
-SECOND_AFTER = 4
+FRONT_BATCHES = 2
 
 FLOPS = 2 * B * L * C * C * TAPS + 2 * OUT * C * B * L * TAPS
 
@@ -41,20 +40,21 @@ def tile_conditionalfeaturesupsample_t_kernel(tc, local_features, wt, bt, w1, b1
         raw_pool = stack.enter_context(tc.tile_pool(name="raw", bufs=RAW_BUFS))
         w_grouped_pool = stack.enter_context(tc.tile_pool(name="w_grouped", bufs=3))
         x_grouped_pool = stack.enter_context(tc.tile_pool(name="x_grouped", bufs=2))
-        planes_pool = stack.enter_context(tc.tile_pool(name="planes", bufs=3))
+        front_pool = stack.enter_context(tc.tile_pool(name="front", bufs=2))
+        planes_pool = stack.enter_context(tc.tile_pool(name="planes", bufs=2))
         up_grouped_pool = stack.enter_context(tc.tile_pool(name="up_grouped", bufs=2 * HALVES))
-        up_codes_pool = stack.enter_context(tc.tile_pool(name="up_codes", bufs=2))
-        y_pool = stack.enter_context(tc.tile_pool(name="y", bufs=3))
+        up_codes_pool = stack.enter_context(tc.tile_pool(name="up_codes", bufs=4))
+        y_pool = stack.enter_context(tc.tile_pool(name="y", bufs=4))
         acc_psum = stack.enter_context(tc.psum_pool(name="acc_psum", bufs=4))
         y_psum = stack.enter_context(tc.psum_pool(name="y_psum", bufs=2))
         tr_psum = stack.enter_context(tc.psum_pool(name="tr_psum", bufs=2))
 
-        ring_order = [("x", 0)]
-        ring_order.extend([("wt", chunk) for chunk in range(W_CHUNKS // 2)])
-        ring_order.append(("x", 1))
-        ring_order.extend([("wt", chunk) for chunk in range(W_CHUNKS // 2, W_CHUNKS)])
+        ring_order = []
+        for i in range(FRONT_BATCHES):
+            ring_order.extend([("wt", i), ("x", i)])
+        ring_order.extend([("wt", chunk) for chunk in range(FRONT_BATCHES, W_CHUNKS)])
         ring_order.append(("w1", 0))
-        ring_order.extend([("x", b) for b in range(2, B)])
+        ring_order.extend([("x", b) for b in range(FRONT_BATCHES, B)])
         raw = {}
 
         def load_next():
@@ -83,23 +83,24 @@ def tile_conditionalfeaturesupsample_t_kernel(tc, local_features, wt, bt, w1, b1
                 nc.sync.dma_start(out=w1_raw[:], in_=w1.rearrange("(n p) c -> p n c", p=P))
                 raw[name, index] = w1_raw
 
-        for slot in range(RAW_BUFS):
-            load_next()
-
         bias_rows = keep.tile([P, P], BF16)
         nc.vector.memset(bias_rows[:], 0.0)
-        nc.scalar.dma_start(out=bias_rows[0:O_TILES, :], in_=bt.rearrange("(t p) -> t p", p=P))
-        nc.scalar.dma_start(
+        load_next()
+        nc.sync.dma_start(out=bias_rows[0:O_TILES, :], in_=bt.rearrange("(t p) -> t p", p=P))
+        nc.sync.dma_start(
             out=bias_rows[O_TILES : O_TILES + OUT_TILES, :], in_=b1.rearrange("(n p) -> n p", p=P)
         )
+
+        for slot in range(RAW_BUFS - 1):
+            load_next()
 
         ident_f32 = keep.tile([P, P], F32)
         make_identity(nc, ident_f32[:])
         ident_bf16 = keep.tile([P, P], BF16)
         make_identity(nc, ident_bf16[:])
 
-        x_codes = keep.tile([P, B, PASSES, L], U32, align_bytes=64)
-        x_scales = keep.tile([P, B, PASSES, L], U8, align_bytes=64)
+        x_codes = keep.tile([P, PASSES, B * L], U32, align_bytes=64)
+        x_scales = keep.tile([P, PASSES, B * L], U8, align_bytes=64)
         w_codes = keep.tile([P, W_CHUNKS, TAPS, W_COLS], U32, align_bytes=64)
         w_scales = keep.tile([P, W_CHUNKS, TAPS, W_COLS], U8, align_bytes=64)
         w1_codes = keep.tile([P, PASSES, OUT], U32, align_bytes=64)
@@ -110,7 +111,7 @@ def tile_conditionalfeaturesupsample_t_kernel(tc, local_features, wt, bt, w1, b1
             x_words = raw["x", b][:].bitcast(F32).rearrange(
                 "p (r h q u) -> p r h u q", r=HALVES, h=PASSES, u=PAIR
             )
-            x_grouped = x_grouped_pool.tile([P, PASSES * L * PACK], BF16, align_bytes=64)
+            x_grouped = x_grouped_pool.tile([P, PASSES * L * PACK], BF16, align_bytes=64, tag="grouped")
             x_grouped_words = x_grouped[:].bitcast(F32).rearrange("p (h r u) -> p h r u", h=PASSES, u=PAIR)
             for h in range(PASSES):
                 x_t = tr_psum.tile([P, PAIR, L], F32, tag="tr")
@@ -121,11 +122,13 @@ def tile_conditionalfeaturesupsample_t_kernel(tc, local_features, wt, bt, w1, b1
                         )
                 nc.scalar.copy(out=x_grouped_words[:, h], in_=x_t[:].rearrange("p u r -> p r u"))
             load_next()
-            nc.vector.quantize_mx(
-                out=x_codes[:, b].rearrange("p h r -> p (h r)").bitcast(FP8X4),
-                scales=x_scales[:, b].rearrange("p h r -> p (h r)"),
-                in_=x_grouped[:],
-            )
+            cols = slice(L * b, L * (b + 1))
+            for h in range(PASSES):
+                nc.vector.quantize_mx(
+                    out=x_codes[:, h, cols].bitcast(FP8X4),
+                    scales=x_scales[:, h, cols],
+                    in_=x_grouped[:, L * PACK * h : L * PACK * (h + 1)],
+                )
 
         def prepare_biases():
             bias_t = tr_psum.tile([P, P], BF16, tag="tr")
@@ -134,7 +137,7 @@ def tile_conditionalfeaturesupsample_t_kernel(tc, local_features, wt, bt, w1, b1
 
         def prepare_w1():
             w1_raw = raw["w1", 0]
-            w1_grouped = keep.tile([P, PASSES, OUT, PACK], BF16, align_bytes=64)
+            w1_grouped = x_grouped_pool.tile([P, PASSES, OUT, PACK], BF16, align_bytes=64, tag="grouped")
             for g in range(PASSES):
                 for n in range(OUT_TILES):
                     w1_t = tr_psum.tile([P, PACK, P], BF16, tag="tr")
@@ -172,11 +175,12 @@ def tile_conditionalfeaturesupsample_t_kernel(tc, local_features, wt, bt, w1, b1
                 in_=w_grouped_of[chunk][:].rearrange("p k o j -> p (k o j)"),
             )
 
-        def first_product(b, first_half, halves, o_tile, planes):
+        def first_product(first_block, offset, blocks, o_tile, planes):
             oc, s = divmod(o_tile, W_TILES)
             o_cols = slice(P * s, P * (s + 1))
-            width = P * halves
-            x_cols = slice(P * first_half, P * first_half + width)
+            width = P * blocks
+            first_col = P * (first_block + offset)
+            x_cols = slice(first_col, first_col + width)
             taps_in_bank = BANK // width
             t = o_tile % PACK
             for k0 in range(0, TAPS, taps_in_bank):
@@ -188,35 +192,46 @@ def tile_conditionalfeaturesupsample_t_kernel(tc, local_features, wt, bt, w1, b1
                             out=acc[:, i, :],
                             lhsT=w_codes[:, chunk, k0 + i, o_cols].bitcast(FP8X4),
                             lhsT_scale=w_scales[:, chunk, k0 + i, o_cols],
-                            rhs=x_codes[:, b, h, x_cols].bitcast(FP8X4),
-                            rhs_scale=x_scales[:, b, h, x_cols],
+                            rhs=x_codes[:, h, x_cols].bitcast(FP8X4),
+                            rhs_scale=x_scales[:, h, x_cols],
                             start=(h == 0),
                             stop=(h == PASSES - 1),
                         )
                 nc.scalar.activation(
-                    out=planes[:, t, :, k0 : k0 + taps_in_bank, :].rearrange("p f k l -> p k f l"),
-                    in_=acc[:].rearrange("p k (f l) -> p k f l", f=halves),
+                    out=planes[:, t, offset : offset + blocks, k0 : k0 + taps_in_bank, :].rearrange("p f k l -> p k f l"),
+                    in_=acc[:].rearrange("p k (f l) -> p k f l", f=blocks),
                     func=IDENTITY,
                     bias=bias_cols[:, o_tile : o_tile + 1],
                 )
 
-        def quantise_up(g, halves, planes, up_codes, up_scales):
-            grouped_halves = []
-            for f in range(halves):
+        up_codes_of = {}
+
+        def new_up(block):
+            up_codes = up_codes_pool.tile([P, PASSES, BANK], U32, align_bytes=64, tag="up_codes")
+            up_scales = up_codes_pool.tile([P, PASSES, BANK], U8, align_bytes=64, tag="up_scales")
+            up_codes_of[block] = (up_codes, up_scales)
+
+        def quantise_up(g, first_block, offset, blocks, planes):
+            grouped = []
+            for f in range(offset, offset + blocks):
+                if g == 0:
+                    new_up(first_block + f)
                 up_grouped = up_grouped_pool.tile([P, BANK, PACK], BF16, align_bytes=64)
                 nc.vector.tensor_copy(
                     out=up_grouped[:].rearrange("p (c i) t -> p c t i", i=RUN),
                     in_=planes[:, :, f].rearrange("p t k l -> p t (k l)").rearrange("p t (c i) -> p c t i", i=RUN),
                 )
-                grouped_halves.append(up_grouped)
-            for f in range(halves):
+                grouped.append(up_grouped)
+            for f in range(offset, offset + blocks):
+                up_codes, up_scales = up_codes_of[first_block + f]
                 nc.vector.quantize_mx(
-                    out=up_codes[:, g, f, :].bitcast(FP8X4),
-                    scales=up_scales[:, g, f, :],
-                    in_=grouped_halves[f][:].rearrange("p c t -> p (c t)"),
+                    out=up_codes[:, g, :].bitcast(FP8X4),
+                    scales=up_scales[:, g, :],
+                    in_=grouped[f - offset][:].rearrange("p c t -> p (c t)"),
                 )
 
-        def second_product(f, up_codes, up_scales, y_sb):
+        def second_product(block, f, y_sb):
+            up_codes, up_scales = up_codes_of[block]
             for n in range(OUT_TILES):
                 y_acc = y_psum.tile([P, TAPS, P], F32, tag="y")
                 for g in range(PASSES):
@@ -224,8 +239,8 @@ def tile_conditionalfeaturesupsample_t_kernel(tc, local_features, wt, bt, w1, b1
                         out=y_acc[:].rearrange("p k l -> p (k l)"),
                         lhsT=w1_codes[:, g, P * n : P * (n + 1)].bitcast(FP8X4),
                         lhsT_scale=w1_scales[:, g, P * n : P * (n + 1)],
-                        rhs=up_codes[:, g, f, :].bitcast(FP8X4),
-                        rhs_scale=up_scales[:, g, f, :],
+                        rhs=up_codes[:, g, :].bitcast(FP8X4),
+                        rhs_scale=up_scales[:, g, :],
                         start=(g == 0),
                         stop=(g == PASSES - 1),
                     )
@@ -237,49 +252,84 @@ def tile_conditionalfeaturesupsample_t_kernel(tc, local_features, wt, bt, w1, b1
                 else:
                     nc.scalar.activation(out=y_out, in_=y_in, func=IDENTITY, bias=y_bias)
 
-        def finish(b, first_half, halves, up_codes, up_scales, y_sb):
-            for f in range(halves):
-                second_product(f, up_codes, up_scales, y_sb)
-            first_t = BANK * first_half
+        def finish(first_block, blocks):
+            y_sb = y_pool.tile([P, OUT_TILES, blocks, BANK], F32, tag="y_sb")
+            for f in range(blocks):
+                second_product(first_block + f, f, y_sb)
+            b, half = divmod(first_block, HALVES)
+            first_t = BANK * half
             for r in range(REPEAT):
                 nc.sync.dma_start(
-                    out=out[:, b, :, T_OUT * r + first_t : T_OUT * r + first_t + BANK * halves],
+                    out=out[:, b, :, T_OUT * r + first_t : T_OUT * r + first_t + BANK * blocks],
                     in_=y_sb[:].rearrange("p n f c -> p n (f c)"),
                 )
 
-        pieces = [(b, 0, HALVES) for b in range(WHOLE_BATCHES)]
-        pieces.extend([(b, half, 1) for b in range(WHOLE_BATCHES, B) for half in range(HALVES)])
-        prepare_x(0)
         prepare_biases()
         group_w(0)
-        unfinished = []
-        for index, (b, first_half, halves) in enumerate(pieces):
-            up_codes = up_codes_pool.tile([P, PASSES, halves, BANK], U32, align_bytes=64, tag="up_codes")
-            up_scales = up_codes_pool.tile([P, PASSES, halves, BANK], U8, align_bytes=64, tag="up_scales")
-            y_sb = y_pool.tile([P, OUT_TILES, halves, BANK], F32, tag="y_sb")
-            planes_of = []
+        prepare_x(0)
+        group_w(1)
+        prepare_x(1)
+        front_blocks = FRONT_BATCHES * HALVES
+        front_planes = []
+        for g in range(PASSES):
+            planes = front_pool.tile([P, PACK, front_blocks, TAPS, P], BF16, tag="front")
+            front_planes.append(planes)
+            for t in range(0, PACK, W_TILES):
+                o_tile = PACK * g + t
+                for h in range(PASSES):
+                    chunk = PASSES * (o_tile // W_TILES) + h
+                    quantise_w(chunk)
+                    if chunk + 2 < W_CHUNKS:
+                        group_w(chunk + 2)
+                if o_tile + W_TILES < O_TILES:
+                    for s in range(W_TILES):
+                        first_product(0, 0, front_blocks, o_tile + s, planes)
+        prepare_w1()
+        for f in range(HALVES):
+            for s in range(W_TILES):
+                first_product(0, f, 1, O_TILES - W_TILES + s, front_planes[1])
+        for s in range(W_TILES):
+            first_product(0, HALVES, HALVES, O_TILES - W_TILES + s, front_planes[1])
+        prepare_x(2)
+
+        def rest_planes(blocks):
+            planes = planes_pool.tile([P, PACK, blocks, TAPS, P], BF16, tag="planes")
+            return planes
+
+        planes = rest_planes(2)
+        quantise_up(0, 0, 0, 1, front_planes[0])
+        quantise_up(1, 0, 0, 1, front_planes[1])
+        quantise_up(0, 0, 1, 1, front_planes[0])
+        finish(0, 1)
+        quantise_up(1, 0, 1, 1, front_planes[1])
+        quantise_up(0, 0, 2, 1, front_planes[0])
+        first_product(4, 0, 2, 0, planes)
+        finish(1, 1)
+        quantise_up(1, 0, 2, 1, front_planes[1])
+        quantise_up(0, 0, 3, 1, front_planes[0])
+        first_product(4, 0, 2, 1, planes)
+        finish(2, 1)
+        first_product(4, 0, 2, 2, planes)
+        quantise_up(1, 0, 3, 1, front_planes[1])
+        first_product(4, 0, 2, 3, planes)
+        prepare_x(3)
+        quantise_up(0, 4, 0, 2, planes)
+        finish(3, 1)
+        planes = rest_planes(2)
+        for t in range(PACK):
+            first_product(4, 0, 2, PACK + t, planes)
+        quantise_up(1, 4, 0, 2, planes)
+        for half in range(HALVES):
+            first = 6 + half
             for g in range(PASSES):
-                planes = planes_pool.tile([P, PACK, halves, TAPS, P], BF16, tag="planes")
-                planes_of.append(planes)
+                planes = rest_planes(1)
                 for t in range(PACK):
-                    o_tile = PACK * g + t
-                    if index == 0 and o_tile % W_TILES == 0:
-                        for h in range(PASSES):
-                            chunk = PASSES * (o_tile // W_TILES) + h
-                            if chunk + 1 < W_CHUNKS:
-                                group_w(chunk + 1)
-                            quantise_w(chunk)
-                    first_product(b, first_half, halves, o_tile, planes)
-                    if index > 0 and o_tile == SECOND_AFTER - 1:
-                        finish(*unfinished.pop())
-                if g == 0 and first_half == 0 and b + 1 < B:
-                    prepare_x(b + 1)
-                if g == 1 and index == 0:
-                    prepare_w1()
-                if index > 0:
-                    quantise_up(g, halves, planes, up_codes, up_scales)
-            if index == 0:
-                for g in range(PASSES):
-                    quantise_up(g, halves, planes_of[g], up_codes, up_scales)
-            unfinished.append((b, first_half, halves, up_codes, up_scales, y_sb))
-        finish(*unfinished.pop())
+                    first_product(first, 0, 1, PACK * g + t, planes)
+                    if g == 0 and t == 1:
+                        if half == 0:
+                            finish(4, 1)
+                            finish(5, 1)
+                        else:
+                            finish(6, 1)
+                quantise_up(g, first, 0, 1, planes)
+        finish(7, 1)

@@ -52,8 +52,9 @@ def tile_conditionalfeaturesupsample_t_kernel(tc, local_features, wt, bt, w1, b1
         ring_order = []
         for i in range(FRONT_BATCHES):
             ring_order.extend([("wt", i), ("x", i)])
-        ring_order.extend([("wt", chunk) for chunk in range(FRONT_BATCHES, W_CHUNKS)])
+        ring_order.extend([("wt", chunk) for chunk in range(FRONT_BATCHES, W_CHUNKS - PASSES)])
         ring_order.append(("w1", 0))
+        ring_order.extend([("wt", chunk) for chunk in range(W_CHUNKS - PASSES, W_CHUNKS)])
         ring_order.extend([("x", b) for b in range(FRONT_BATCHES, B)])
         raw = {}
 
@@ -198,7 +199,7 @@ def tile_conditionalfeaturesupsample_t_kernel(tc, local_features, wt, bt, w1, b1
                             stop=(h == PASSES - 1),
                         )
                 nc.scalar.activation(
-                    out=planes[:, t, offset : offset + blocks, k0 : k0 + taps_in_bank, :].rearrange("p f k l -> p k f l"),
+                    out=planes[:, offset : offset + blocks, t, k0 : k0 + taps_in_bank, :].rearrange("p f k l -> p k f l"),
                     in_=acc[:].rearrange("p k (f l) -> p k f l", f=blocks),
                     func=IDENTITY,
                     bias=bias_cols[:, o_tile : o_tile + 1],
@@ -219,7 +220,7 @@ def tile_conditionalfeaturesupsample_t_kernel(tc, local_features, wt, bt, w1, b1
                 up_grouped = up_grouped_pool.tile([P, BANK, PACK], BF16, align_bytes=64)
                 nc.vector.tensor_copy(
                     out=up_grouped[:].rearrange("p (c i) t -> p c t i", i=RUN),
-                    in_=planes[:, :, f].rearrange("p t k l -> p t (k l)").rearrange("p t (c i) -> p c t i", i=RUN),
+                    in_=planes[:, f].rearrange("p t k l -> p t (k l)").rearrange("p t (c i) -> p c t i", i=RUN),
                 )
                 grouped.append(up_grouped)
             for f in range(offset, offset + blocks):
@@ -272,7 +273,7 @@ def tile_conditionalfeaturesupsample_t_kernel(tc, local_features, wt, bt, w1, b1
         front_blocks = FRONT_BATCHES * HALVES
         front_planes = []
         for g in range(PASSES):
-            planes = front_pool.tile([P, PACK, front_blocks, TAPS, P], BF16, tag="front")
+            planes = front_pool.tile([P, front_blocks, PACK, TAPS, P], BF16, tag="front")
             front_planes.append(planes)
             for t in range(0, PACK, W_TILES):
                 o_tile = PACK * g + t
@@ -284,32 +285,33 @@ def tile_conditionalfeaturesupsample_t_kernel(tc, local_features, wt, bt, w1, b1
                 if o_tile + W_TILES < O_TILES:
                     for s in range(W_TILES):
                         first_product(0, 0, front_blocks, o_tile + s, planes)
-        prepare_w1()
+                if o_tile == PACK - W_TILES:
+                    prepare_w1()
         for f in range(HALVES):
             for s in range(W_TILES):
                 first_product(0, f, 1, O_TILES - W_TILES + s, front_planes[1])
         for s in range(W_TILES):
             first_product(0, HALVES, HALVES, O_TILES - W_TILES + s, front_planes[1])
-        prepare_x(2)
 
         def rest_planes(blocks):
-            planes = planes_pool.tile([P, PACK, blocks, TAPS, P], BF16, tag="planes")
+            planes = planes_pool.tile([P, blocks, PACK, TAPS, P], BF16, tag="planes")
             return planes
 
         planes = rest_planes(2)
         quantise_up(0, 0, 0, 1, front_planes[0])
         quantise_up(1, 0, 0, 1, front_planes[1])
-        quantise_up(0, 0, 1, 1, front_planes[0])
         finish(0, 1)
+        quantise_up(0, 0, 1, 1, front_planes[0])
         quantise_up(1, 0, 1, 1, front_planes[1])
-        quantise_up(0, 0, 2, 1, front_planes[0])
-        first_product(4, 0, 2, 0, planes)
+        prepare_x(2)
         finish(1, 1)
+        quantise_up(0, 0, 2, 1, front_planes[0])
         quantise_up(1, 0, 2, 1, front_planes[1])
-        quantise_up(0, 0, 3, 1, front_planes[0])
+        first_product(4, 0, 2, 0, planes)
         first_product(4, 0, 2, 1, planes)
         finish(2, 1)
         first_product(4, 0, 2, 2, planes)
+        quantise_up(0, 0, 3, 1, front_planes[0])
         quantise_up(1, 0, 3, 1, front_planes[1])
         first_product(4, 0, 2, 3, planes)
         prepare_x(3)

@@ -41,7 +41,7 @@ def tile_conditionalfeaturesupsample_t_kernel(tc, local_features, wt, bt, w1, b1
         w_grouped_pool = stack.enter_context(tc.tile_pool(name="w_grouped", bufs=3))
         x_grouped_pool = stack.enter_context(tc.tile_pool(name="x_grouped", bufs=2))
         front_pool = stack.enter_context(tc.tile_pool(name="front", bufs=2))
-        planes_pool = stack.enter_context(tc.tile_pool(name="planes", bufs=2))
+        planes_pool = stack.enter_context(tc.tile_pool(name="planes", bufs=4))
         up_grouped_pool = stack.enter_context(tc.tile_pool(name="up_grouped", bufs=2 * HALVES))
         up_codes_pool = stack.enter_context(tc.tile_pool(name="up_codes", bufs=4))
         y_pool = stack.enter_context(tc.tile_pool(name="y", bufs=4))
@@ -212,24 +212,25 @@ def tile_conditionalfeaturesupsample_t_kernel(tc, local_features, wt, bt, w1, b1
             up_scales = up_codes_pool.tile([P, PASSES, BANK], U8, align_bytes=64, tag="up_scales")
             up_codes_of[block] = (up_codes, up_scales)
 
-        def quantise_up(g, first_block, offset, blocks, planes):
-            grouped = []
-            for f in range(offset, offset + blocks):
-                if g == 0:
-                    new_up(first_block + f)
-                up_grouped = up_grouped_pool.tile([P, BANK, PACK], BF16, align_bytes=64)
-                nc.vector.tensor_copy(
-                    out=up_grouped[:].rearrange("p (c i) t -> p c t i", i=RUN),
-                    in_=planes[:, f].rearrange("p t k l -> p t (k l)").rearrange("p t (c i) -> p c t i", i=RUN),
-                )
-                grouped.append(up_grouped)
-            for f in range(offset, offset + blocks):
-                up_codes, up_scales = up_codes_of[first_block + f]
-                nc.vector.quantize_mx(
-                    out=up_codes[:, g, :].bitcast(FP8X4),
-                    scales=up_scales[:, g, :],
-                    in_=grouped[f - offset][:].rearrange("p c t -> p (c t)"),
-                )
+        up_grouped_of = {}
+
+        def regroup_up(g, block, f, planes):
+            up_grouped = up_grouped_pool.tile([P, BANK, PACK], BF16, align_bytes=64)
+            nc.vector.tensor_copy(
+                out=up_grouped[:].rearrange("p (c i) t -> p c t i", i=RUN),
+                in_=planes[:, f].rearrange("p t k l -> p t (k l)").rearrange("p t (c i) -> p c t i", i=RUN),
+            )
+            up_grouped_of[g, block] = up_grouped
+
+        def quantise_up(g, block):
+            if g == 0:
+                new_up(block)
+            up_codes, up_scales = up_codes_of[block]
+            nc.vector.quantize_mx(
+                out=up_codes[:, g, :].bitcast(FP8X4),
+                scales=up_scales[:, g, :],
+                in_=up_grouped_of[g, block][:].rearrange("p c t -> p (c t)"),
+            )
 
         def second_product(block, f, y_sb):
             up_codes, up_scales = up_codes_of[block]
@@ -284,54 +285,42 @@ def tile_conditionalfeaturesupsample_t_kernel(tc, local_features, wt, bt, w1, b1
                         group_w(chunk + 2)
                 if o_tile + W_TILES < O_TILES:
                     for s in range(W_TILES):
-                        first_product(0, 0, front_blocks, o_tile + s, planes)
+                        first_product(0, 0, HALVES if g else front_blocks, o_tile + s, planes)
                 if o_tile == PACK - W_TILES:
                     prepare_w1()
         for f in range(HALVES):
             for s in range(W_TILES):
                 first_product(0, f, 1, O_TILES - W_TILES + s, front_planes[1])
-        for s in range(W_TILES):
-            first_product(0, HALVES, HALVES, O_TILES - W_TILES + s, front_planes[1])
 
-        def rest_planes(blocks):
-            planes = planes_pool.tile([P, blocks, PACK, TAPS, P], BF16, tag="planes")
-            return planes
+        low, high = front_planes
 
-        planes = rest_planes(2)
-        quantise_up(0, 0, 0, 1, front_planes[0])
-        quantise_up(1, 0, 0, 1, front_planes[1])
+        def both_passes(block):
+            regroup_up(0, block, block, low)
+            regroup_up(1, block, block, high)
+            quantise_up(0, block)
+            quantise_up(1, block)
+
+        both_passes(0)
+        first_product(0, HALVES, HALVES, PACK, high)
         finish(0, 1)
-        quantise_up(0, 0, 1, 1, front_planes[0])
-        quantise_up(1, 0, 1, 1, front_planes[1])
-        prepare_x(2)
+        both_passes(1)
+        for t in range(1, PACK):
+            first_product(0, HALVES, HALVES, PACK + t, high)
         finish(1, 1)
-        quantise_up(0, 0, 2, 1, front_planes[0])
-        quantise_up(1, 0, 2, 1, front_planes[1])
-        first_product(4, 0, 2, 0, planes)
-        first_product(4, 0, 2, 1, planes)
-        finish(2, 1)
-        first_product(4, 0, 2, 2, planes)
-        quantise_up(0, 0, 3, 1, front_planes[0])
-        quantise_up(1, 0, 3, 1, front_planes[1])
-        first_product(4, 0, 2, 3, planes)
-        prepare_x(3)
-        quantise_up(0, 4, 0, 2, planes)
-        finish(3, 1)
-        planes = rest_planes(2)
-        for t in range(PACK):
-            first_product(4, 0, 2, PACK + t, planes)
-        quantise_up(1, 4, 0, 2, planes)
-        for half in range(HALVES):
-            first = 6 + half
+        prepare_x(2)
+        both_passes(2)
+        for block in range(4, 8):
             for g in range(PASSES):
-                planes = rest_planes(1)
+                planes = planes_pool.tile([P, 1, PACK, TAPS, P], BF16, tag="planes")
                 for t in range(PACK):
-                    first_product(first, 0, 1, PACK * g + t, planes)
-                    if g == 0 and t == 1:
-                        if half == 0:
-                            finish(4, 1)
-                            finish(5, 1)
-                        else:
-                            finish(6, 1)
-                quantise_up(g, first, 0, 1, planes)
+                    first_product(block, 0, 1, PACK * g + t, planes)
+                    if block == 4 and g == 0 and t == 1:
+                        finish(2, 1)
+                        both_passes(3)
+                    if g == 1 and t == 1:
+                        finish(block - 1, 1)
+                regroup_up(g, block, 0, planes)
+                quantise_up(g, block)
+            if block == 4:
+                prepare_x(3)
         finish(7, 1)

@@ -216,10 +216,13 @@ def tile_conditionalfeaturesupsample_t_kernel(tc, local_features, wt, bt, w1, b1
 
         def regroup_up(g, block, f, planes):
             up_grouped = up_grouped_pool.tile([P, BANK, PACK], BF16, align_bytes=64)
-            nc.vector.tensor_copy(
-                out=up_grouped[:].rearrange("p (c i) t -> p c t i", i=RUN),
-                in_=planes[:, f].rearrange("p t k l -> p t (k l)").rearrange("p t (c i) -> p c t i", i=RUN),
-            )
+            shared = (g, block) == (PASSES - 1, 7)
+            split = BANK // RUN - (BANK // RUN // 3 if shared else 0)
+            target = up_grouped[:].rearrange("p (c i) t -> p c t i", i=RUN)
+            source = planes[:, f].rearrange("p t k l -> p t (k l)").rearrange("p t (c i) -> p c t i", i=RUN)
+            nc.vector.tensor_copy(out=target[:, :split], in_=source[:, :split])
+            if shared:
+                nc.scalar.copy(out=target[:, split:], in_=source[:, split:])
             up_grouped_of[g, block] = up_grouped
 
         def quantise_up(g, block):
@@ -260,11 +263,13 @@ def tile_conditionalfeaturesupsample_t_kernel(tc, local_features, wt, bt, w1, b1
                 second_product(first_block + f, f, y_sb)
             b, half = divmod(first_block, HALVES)
             first_t = BANK * half
-            for r in range(REPEAT):
-                nc.sync.dma_start(
-                    out=out[:, b, :, T_OUT * r + first_t : T_OUT * r + first_t + BANK * blocks],
-                    in_=y_sb[:].rearrange("p n f c -> p n (f c)"),
-                )
+            groups = [slice(n, n + 1) for n in range(OUT_TILES)] if first_block == 7 else [slice(0, OUT_TILES)]
+            for group in groups:
+                for r in range(REPEAT):
+                    nc.sync.dma_start(
+                        out=out[:, b, group, T_OUT * r + first_t : T_OUT * r + first_t + BANK * blocks],
+                        in_=y_sb[:, group].rearrange("p n f c -> p n (f c)"),
+                    )
 
         prepare_biases()
         group_w(0)

from contextlib import ExitStack

import concourse.mybir as mybir
from concourse.masks import make_identity

F32 = mybir.dt.float32
BF16 = mybir.dt.bfloat16
U32 = mybir.dt.uint32
U8 = mybir.dt.uint8
FP8X4 = mybir.dt.float8_e4m3fn_x4
IDENTITY = mybir.ActivationFunctionType.Identity

B, L, C, TAPS, OUT, REPEAT = 4, 256, 1024, 4, 256, 4
T_OUT = L * TAPS
P = 128
PACK = 4
PAIR = 2
K_PASS = P * PACK
PASSES = C // K_PASS
BANK = 512
O_TILES = C // P
OUT_TILES = OUT // P
HALVES = L // P
W_COLS = 256
W_TILES = W_COLS // P
W_CHUNKS = (C // W_COLS) * PASSES
RUN = 4

W_SCALAR_COLS = 48
RAW_BUFS = 6
FRONT_BATCHES = 2

FLOPS = 2 * B * L * C * C * TAPS + 2 * OUT * C * B * L * TAPS


def tile_conditionalfeaturesupsample_t_kernel(tc, local_features, wt, bt, w1, b1, out):
    nc = tc.nc
    with ExitStack() as stack:
        keep = stack.enter_context(tc.tile_pool(name="keep", bufs=1))
        raw_pool = stack.enter_context(tc.tile_pool(name="raw", bufs=RAW_BUFS))
        w_grouped_pool = stack.enter_context(tc.tile_pool(name="w_grouped", bufs=3))
        x_grouped_pool = stack.enter_context(tc.tile_pool(name="x_grouped", bufs=2))
        front_pool = stack.enter_context(tc.tile_pool(name="front", bufs=2))
        planes_pool = stack.enter_context(tc.tile_pool(name="planes", bufs=4))
        up_grouped_pool = stack.enter_context(tc.tile_pool(name="up_grouped", bufs=2 * HALVES))
        up_codes_pool = stack.enter_context(tc.tile_pool(name="up_codes", bufs=4))
        y_pool = stack.enter_context(tc.tile_pool(name="y", bufs=4))
        acc_psum = stack.enter_context(tc.psum_pool(name="acc_psum", bufs=4))
        y_psum = stack.enter_context(tc.psum_pool(name="y_psum", bufs=2))
        tr_psum = stack.enter_context(tc.psum_pool(name="tr_psum", bufs=2))

        ring_order = []
        for i in range(FRONT_BATCHES):
            ring_order.extend([("wt", i), ("x", i)])
        ring_order.extend([("wt", chunk) for chunk in range(FRONT_BATCHES, W_CHUNKS - PASSES)])
        ring_order.append(("w1", 0))
        ring_order.extend([("wt", chunk) for chunk in range(W_CHUNKS - PASSES, W_CHUNKS)])
        ring_order.extend([("x", b) for b in range(FRONT_BATCHES, B)])
        raw = {}

        def load_next():
            if len(raw) == len(ring_order):
                return
            name, index = ring_order[len(raw)]
            if name == "x":
                x_raw = raw_pool.tile([P, HALVES * C], BF16, tag="raw")
                nc.sync.dma_start(
                    out=x_raw[:].rearrange("p (r c) -> p r c", r=HALVES),
                    in_=local_features[index].rearrange("(r p) c -> p r c", p=P),
                )
                raw[name, index] = x_raw
            elif name == "wt":
                oc, h = divmod(index, PASSES)
                w_raw = raw_pool.tile([P, PACK, W_COLS * TAPS], BF16, tag="raw")
                nc.sync.dma_start(
                    out=w_raw[:],
                    in_=wt[K_PASS * h : K_PASS * (h + 1), W_COLS * oc : W_COLS * (oc + 1), :].rearrange(
                        "(p j) o k -> p j (o k)", j=PACK
                    ),
                )
                raw[name, index] = w_raw
            else:
                w1_raw = raw_pool.tile([P, OUT_TILES, C], BF16, tag="raw")
                nc.sync.dma_start(out=w1_raw[:], in_=w1.rearrange("(n p) c -> p n c", p=P))
                raw[name, index] = w1_raw

        bias_rows = keep.tile([P, P], BF16)
        nc.vector.memset(bias_rows[:], 0.0)
        load_next()
        nc.sync.dma_start(out=bias_rows[0:O_TILES, :], in_=bt.rearrange("(t p) -> t p", p=P))
        nc.sync.dma_start(
            out=bias_rows[O_TILES : O_TILES + OUT_TILES, :], in_=b1.rearrange("(n p) -> n p", p=P)
        )

        for slot in range(RAW_BUFS - 1):
            load_next()

        ident_f32 = keep.tile([P, P], F32)
        make_identity(nc, ident_f32[:])
        ident_bf16 = keep.tile([P, P], BF16)
        make_identity(nc, ident_bf16[:])

        x_codes = keep.tile([P, PASSES, B * L], U32, align_bytes=64)
        x_scales = keep.tile([P, PASSES, B * L], U8, align_bytes=64)
        w_codes = keep.tile([P, W_CHUNKS, TAPS, W_COLS], U32, align_bytes=64)
        w_scales = keep.tile([P, W_CHUNKS, TAPS, W_COLS], U8, align_bytes=64)
        w1_codes = keep.tile([P, PASSES, OUT], U32, align_bytes=64)
        w1_scales = keep.tile([P, PASSES, OUT], U8, align_bytes=64)
        bias_cols = keep.tile([P, O_TILES + OUT_TILES], F32)

        def prepare_x(b):
            x_words = raw["x", b][:].bitcast(F32).rearrange(
                "p (r h q u) -> p r h u q", r=HALVES, h=PASSES, u=PAIR
            )
            x_grouped = x_grouped_pool.tile([P, PASSES * L * PACK], BF16, align_bytes=64, tag="grouped")
            x_grouped_words = x_grouped[:].bitcast(F32).rearrange("p (h r u) -> p h r u", h=PASSES, u=PAIR)
            for h in range(PASSES):
                x_t = tr_psum.tile([P, PAIR, L], F32, tag="tr")
                for u in range(PAIR):
                    for r in range(HALVES):
                        nc.tensor.transpose(
                            out=x_t[:, u, P * r : P * (r + 1)], in_=x_words[:, r, h, u, :], identity=ident_f32[:]
                        )
                nc.scalar.copy(out=x_grouped_words[:, h], in_=x_t[:].rearrange("p u r -> p r u"))
            load_next()
            cols = slice(L * b, L * (b + 1))
            for h in range(PASSES):
                nc.vector.quantize_mx(
                    out=x_codes[:, h, cols].bitcast(FP8X4),
                    scales=x_scales[:, h, cols],
                    in_=x_grouped[:, L * PACK * h : L * PACK * (h + 1)],
                )

        def prepare_biases():
            bias_t = tr_psum.tile([P, P], BF16, tag="tr")
            nc.tensor.transpose(out=bias_t[:], in_=bias_rows[:], identity=ident_bf16[:])
            nc.vector.tensor_copy(out=bias_cols[:], in_=bias_t[:, 0 : O_TILES + OUT_TILES])

        def prepare_w1():
            w1_raw = raw["w1", 0]
            w1_grouped = x_grouped_pool.tile([P, PASSES, OUT, PACK], BF16, align_bytes=64, tag="grouped")
            for g in range(PASSES):
                for n in range(OUT_TILES):
                    w1_t = tr_psum.tile([P, PACK, P], BF16, tag="tr")
                    for t in range(PACK):
                        first_o = K_PASS * g + P * t
                        nc.tensor.transpose(
                            out=w1_t[:, t, :], in_=w1_raw[:, n, first_o : first_o + P], identity=ident_bf16[:]
                        )
                    nc.scalar.copy(
                        out=w1_grouped[:, g, P * n : P * (n + 1), :], in_=w1_t[:].rearrange("p t r -> p r t")
                    )
            load_next()
            nc.vector.quantize_mx(
                out=w1_codes[:].rearrange("p g r -> p (g r)").bitcast(FP8X4),
                scales=w1_scales[:].rearrange("p g r -> p (g r)"),
                in_=w1_grouped[:].rearrange("p g r t -> p (g r t)"),
            )

        w_grouped_of = {}

        def group_w(chunk):
            source = raw["wt", chunk][:].rearrange("p j (o k) -> p o j k", k=TAPS)
            w_grouped = w_grouped_pool.tile([P, TAPS, W_COLS, PACK], BF16, align_bytes=64)
            target = w_grouped[:].rearrange("p k o j -> p o j k")
            split = W_COLS - W_SCALAR_COLS
            nc.vector.tensor_copy(out=target[:, :split], in_=source[:, :split])
            nc.scalar.copy(out=target[:, split:], in_=source[:, split:])
            w_grouped_of[chunk] = w_grouped
            load_next()

        def quantise_w(chunk):
            nc.vector.quantize_mx(
                out=w_codes[:, chunk].rearrange("p k o -> p (k o)").bitcast(FP8X4),
                scales=w_scales[:, chunk].rearrange("p k o -> p (k o)"),
                in_=w_grouped_of[chunk][:].rearrange("p k o j -> p (k o j)"),
            )

        def first_product(first_block, offset, blocks, o_tile, planes):
            oc, s = divmod(o_tile, W_TILES)
            o_cols = slice(P * s, P * (s + 1))
            width = P * blocks
            first_col = P * (first_block + offset)
            x_cols = slice(first_col, first_col + width)
            taps_in_bank = BANK // width
            t = o_tile % PACK
            for k0 in range(0, TAPS, taps_in_bank):
                acc = acc_psum.tile([P, taps_in_bank, width], F32, tag="acc")
                for i in range(taps_in_bank):
                    for h in range(PASSES):
                        chunk = PASSES * oc + h
                        nc.tensor.matmul_mx(
                            out=acc[:, i, :],
                            lhsT=w_codes[:, chunk, k0 + i, o_cols].bitcast(FP8X4),
                            lhsT_scale=w_scales[:, chunk, k0 + i, o_cols],
                            rhs=x_codes[:, h, x_cols].bitcast(FP8X4),
                            rhs_scale=x_scales[:, h, x_cols],
                            start=(h == 0),
                            stop=(h == PASSES - 1),
                        )
                nc.scalar.activation(
                    out=planes[:, offset : offset + blocks, t, k0 : k0 + taps_in_bank, :].rearrange("p f k l -> p k f l"),
                    in_=acc[:].rearrange("p k (f l) -> p k f l", f=blocks),
                    func=IDENTITY,
                    bias=bias_cols[:, o_tile : o_tile + 1],
                )

        up_codes_of = {}

        def new_up(block):
            up_codes = up_codes_pool.tile([P, PASSES, BANK], U32, align_bytes=64, tag="up_codes")
            up_scales = up_codes_pool.tile([P, PASSES, BANK], U8, align_bytes=64, tag="up_scales")
            up_codes_of[block] = (up_codes, up_scales)

        up_grouped_of = {}

        def regroup_up(g, block, f, planes):
            up_grouped = up_grouped_pool.tile([P, BANK, PACK], BF16, align_bytes=64)
            shared = (g, block) == (PASSES - 1, 7)
            split = BANK // RUN - (BANK // RUN // 3 if shared else 0)
            target = up_grouped[:].rearrange("p (c i) t -> p c t i", i=RUN)
            source = planes[:, f].rearrange("p t k l -> p t (k l)").rearrange("p t (c i) -> p c t i", i=RUN)
            nc.vector.tensor_copy(out=target[:, :split], in_=source[:, :split])
            if shared:
                nc.scalar.copy(out=target[:, split:], in_=source[:, split:])
            up_grouped_of[g, block] = up_grouped

        def quantise_up(g, block):
            if g == 0:
                new_up(block)
            up_codes, up_scales = up_codes_of[block]
            nc.vector.quantize_mx(
                out=up_codes[:, g, :].bitcast(FP8X4),
                scales=up_scales[:, g, :],
                in_=up_grouped_of[g, block][:].rearrange("p c t -> p (c t)"),
            )

        def second_product(block, f, y_sb):
            up_codes, up_scales = up_codes_of[block]
            for n in range(OUT_TILES):
                y_acc = y_psum.tile([P, TAPS, P], F32, tag="y")
                for g in range(PASSES):
                    nc.tensor.matmul_mx(
                        out=y_acc[:].rearrange("p k l -> p (k l)"),
                        lhsT=w1_codes[:, g, P * n : P * (n + 1)].bitcast(FP8X4),
                        lhsT_scale=w1_scales[:, g, P * n : P * (n + 1)],
                        rhs=up_codes[:, g, :].bitcast(FP8X4),
                        rhs_scale=up_scales[:, g, :],
                        start=(g == 0),
                        stop=(g == PASSES - 1),
                    )
                y_out = y_sb[:, n, f].rearrange("p (l k) -> p l k", k=TAPS)
                y_in = y_acc[:].rearrange("p k l -> p l k")
                y_bias = bias_cols[:, O_TILES + n : O_TILES + n + 1]
                if n % 2 == 0:
                    nc.vector.tensor_scalar_add(out=y_out, in0=y_in, scalar1=y_bias)
                else:
                    nc.scalar.activation(out=y_out, in_=y_in, func=IDENTITY, bias=y_bias)

        def finish(first_block, blocks):
            y_sb = y_pool.tile([P, OUT_TILES, blocks, BANK], F32, tag="y_sb")
            for f in range(blocks):
                second_product(first_block + f, f, y_sb)
            b, half = divmod(first_block, HALVES)
            first_t = BANK * half
            groups = [slice(n, n + 1) for n in range(OUT_TILES)] if first_block == 7 else [slice(0, OUT_TILES)]
            for group in groups:
                for r in range(REPEAT):
                    nc.sync.dma_start(
                        out=out[:, b, group, T_OUT * r + first_t : T_OUT * r + first_t + BANK * blocks],
                        in_=y_sb[:, group].rearrange("p n f c -> p n (f c)"),
                    )

        prepare_biases()
        group_w(0)
        prepare_x(0)
        group_w(1)
        prepare_x(1)
        front_blocks = FRONT_BATCHES * HALVES
        front_planes = []
        for g in range(PASSES):
            planes = front_pool.tile([P, front_blocks, PACK, TAPS, P], BF16, tag="front")
            front_planes.append(planes)
            for t in range(0, PACK, W_TILES):
                o_tile = PACK * g + t
                for h in range(PASSES):
                    chunk = PASSES * (o_tile // W_TILES) + h
                    quantise_w(chunk)
                    if chunk + 2 < W_CHUNKS:
                        group_w(chunk + 2)
                if o_tile + W_TILES < O_TILES:
                    for s in range(W_TILES):
                        first_product(0, 0, HALVES if g else front_blocks, o_tile + s, planes)
                if o_tile == PACK - W_TILES:
                    prepare_w1()
        for f in range(HALVES):
            for s in range(W_TILES):
                first_product(0, f, 1, O_TILES - W_TILES + s, front_planes[1])

        low, high = front_planes

        def both_passes(block):
            regroup_up(0, block, block, low)
            regroup_up(1, block, block, high)
            quantise_up(0, block)
            quantise_up(1, block)

        both_passes(0)
        first_product(0, HALVES, HALVES, PACK, high)
        finish(0, 1)
        both_passes(1)
        for t in range(1, PACK):
            first_product(0, HALVES, HALVES, PACK + t, high)
        finish(1, 1)
        prepare_x(2)
        both_passes(2)
        for block in range(4, 8):
            for g in range(PASSES):
                planes = planes_pool.tile([P, 1, PACK, TAPS, P], BF16, tag="planes")
                for t in range(PACK):
                    first_product(block, 0, 1, PACK * g + t, planes)
                    if block == 4 and g == 0 and t == 1:
                        finish(2, 1)
                        both_passes(3)
                    if g == 1 and t == 1:
                        finish(block - 1, 1)
                regroup_up(g, block, 0, planes)
                quantise_up(g, block)
            if block == 4:
                prepare_x(3)
        finish(7, 1)
